import numpy as np
import ml_dtypes


BF16 = ml_dtypes.bfloat16


def bf(x):
    return np.asarray(x, np.float32).astype(BF16)


def f64(x):
    return np.asarray(x).astype(np.float64)


E2M1 = np.array([0.0, 0.5, 1.0, 1.5, 2.0, 3.0, 4.0, 6.0, -0.0, -0.5, -1.0, -1.5, -2.0, -3.0, -4.0, -6.0])


def pack_weight(w, fmt):
    k, n = w.shape
    w = f64(bf(w)).reshape(k // 32, 32, n)
    amax = np.abs(w).max(1)
    if fmt == "e4m3":
        byte = np.frexp(amax)[1] - 1 + 127 - 7
    else:
        mant, ex = np.frexp(amax / 6.0)
        byte = np.where(mant > 0.5, ex, ex - 1) + 127
    byte = np.clip(np.where(amax > 0, byte, 1), 1, 254)
    scaled = (w * np.exp2(127.0 - byte)[:, None, :]).reshape(k, n).astype(np.float32)
    by_word = np.ascontiguousarray(scaled.reshape(k // 512, 128, 4, n).transpose(0, 1, 3, 2))
    if fmt == "e4m3":
        words = by_word.astype(ml_dtypes.float8_e4m3fn).view(np.uint8)
    else:
        c = by_word.astype(ml_dtypes.float4_e2m1fn).view(np.uint8) & 0xF
        words = c[..., 0::2] | (c[..., 1::2] << 4)
    return np.ascontiguousarray(words), np.ascontiguousarray(byte.astype(np.uint8).reshape(k // 512, 16, n))


def unpack_weight(words, scales, fmt):
    g, p, n, _ = words.shape
    if fmt == "e4m3":
        vals = np.ascontiguousarray(words).view(ml_dtypes.float8_e4m3fn).astype(np.float64)
    else:
        nib = np.empty((g, p, n, 4), np.uint8)
        nib[..., 0::2] = words & 0xF
        nib[..., 1::2] = words >> 4
        vals = E2M1[nib]
    vals = vals * np.repeat(np.exp2(scales.astype(np.float64) - 127.0), 8, axis=1)[..., None]
    return vals.transpose(0, 1, 3, 2).reshape(g * 512, n)

def pack4(w):
    words, scales = pack_weight(w, "e2m1")
    return words.reshape(words.shape[0], 128, -1), scales


def unpack4(words, scales):
    return unpack_weight(words.reshape(words.shape[0], 128, -1, 2), scales, "e2m1")


def kspread(k):
    return np.exp2(np.repeat(np.random.randint(-6, 7, k // 32), 32).astype(np.float64))


B, T, C, H = 2, 64, 4096, 16
D = C // H
ROPE_BASE = 10000.0


def rope_cos_sin():
    inv_freq = 1.0 / (ROPE_BASE ** (np.arange(0, D, 2) / D))
    freqs = np.outer(np.arange(T) * 1.0, inv_freq)
    emb = np.concatenate([freqs, freqs], axis=-1)
    return np.cos(emb), np.sin(emb)


def rotate_half(v):
    v1, v2 = np.split(v, 2, axis=-1)
    return np.concatenate([-v2, v1], axis=-1)


def apply_rotary(v, cos, sin):
    return v * cos[None, None] + rotate_half(v) * sin[None, None]


def setup_inputs():
    s = kspread(C)
    x = np.random.standard_normal((B, T, C)) * s
    x_words, x_scales = pack4(x.reshape(B * T, C).T)
    words, scales = pack4(np.random.standard_normal((C, 2 * C)) / np.sqrt(C) / s[:, None])
    b_qk = bf(np.random.standard_normal(2 * C) * 0.3)
    return {"x_words": x_words, "x_scales": x_scales, "W_qk_words": words, "W_qk_scales": scales, "b_qk": b_qk}


def reference(x_words, x_scales, W_qk_words, W_qk_scales, b_qk):
    xq = unpack4(x_words, x_scales).T.reshape(B, T, C)
    qk = (xq @ unpack4(W_qk_words, W_qk_scales)) + f64(b_qk)
    q, k = np.split(qk, 2, axis=2)
    q = q.reshape(B, T, H, D).transpose(0, 2, 1, 3)
    k = k.reshape(B, T, H, D).transpose(0, 2, 1, 3)
    cos, sin = rope_cos_sin()
    return apply_rotary(q, cos, sin), apply_rotary(k, cos, sin)

@@ -1,0 +1,259 @@
+from contextlib import ExitStack
+
+import concourse.mybir as mybir
+from concourse.masks import make_identity
+
+F32 = mybir.dt.float32
+BF16 = mybir.dt.bfloat16
+I32 = mybir.dt.int32
+U8 = mybir.dt.uint8
+FP4X4 = mybir.dt.float4_e2m1fn_x4
+ALU = mybir.AluOpType
+ACT = mybir.ActivationFunctionType
+
+P = 128
+PASSES = 8
+C_OUT = 8192
+HALF_OUT = 4096
+HEAD = 256
+HALF = 128
+BANK = 512
+GROUP = 2048
+T = 64
+PI = 3.141592653589793
+ROPE_BASE = 10000.0
+
+FLOPS = 2 * 128 * 4096 * 8192
+
+CHUNKS = (
+    (0, 2048, 2),
+    (2048, 2048, 2),
+    (4096, 2048, 2),
+    (6144, 1024, 4),
+    (7168, 512, 4),
+    (7680, 256, 8),
+    (7936, 256, 4),
+)
+CHUNK_POOL = (0, 1, 0, 1, 1, 1, 0)
+LAST_ON_HW_QUEUES = 2
+
+
+def tile_causalselfattention_pa_kernel(
+    tc, x_words, x_scales, W_qk_words, W_qk_scales, b_qk, out_0, out_1
+):
+    nc = tc.nc
+    with ExitStack() as ctx:
+        const = ctx.enter_context(tc.tile_pool(name="const", bufs=1))
+        codes = ctx.enter_context(tc.tile_pool(name="codes", bufs=12))
+        work = ctx.enter_context(tc.tile_pool(name="work", bufs=4))
+        psum_a = ctx.enter_context(tc.psum_pool(name="psum_a", bufs=4))
+        psum_b = ctx.enter_context(tc.psum_pool(name="psum_b", bufs=4))
+        psum = (psum_a, psum_b)
+        ctx.enter_context(tc.manual_schedule())
+
+        bias_rows = const.tile([P, BANK], BF16, name="bias_rows")
+        nc.vector.memset(bias_rows[:], 0.0)
+        nc.scalar.dma_start(out=bias_rows[0:16, :], in_=b_qk.rearrange("(a n) -> a n", a=16))
+        zero_col = const.tile([P, 1], F32, name="zero_col")
+        nc.vector.memset(zero_col[:], 0.0)
+        warm = const.tile([P, 1], F32, name="warm")
+        nc.scalar.activation(out=warm[:], in_=zero_col[:], func=ACT.Sin)
+
+        ident = const.tile([P, P], BF16, name="ident")
+        make_identity(nc, ident[:])
+        pos_i = const.tile([P, 1], I32, name="pos_i")
+        nc.gpsimd.iota(pos_i[0:T, :], pattern=[[1, 1]], base=0, channel_multiplier=1)
+        nc.gpsimd.iota(pos_i[T:P, :], pattern=[[1, 1]], base=0, channel_multiplier=1)
+
+        x_codes = const.tile([P, PASSES, 2 * P], U8, name="x_codes", align_bytes=64)
+        x_plane = const.tile([P, PASSES, P], U8, name="x_plane", align_bytes=64)
+        planes = (
+            const.tile([P, PASSES, GROUP], U8, name="plane0", align_bytes=64),
+            const.tile([P, PASSES, GROUP], U8, name="plane1", align_bytes=64),
+        )
+        xs_view = x_scales.rearrange("g (q r) n -> r q g n", r=4)
+        ws_view = W_qk_scales.rearrange("g (q r) n -> r q g n", r=4)
+
+        def load_scales(group):
+            plane = planes[group % 2]
+            for r in range(4):
+                nc.sync.dma_start(
+                    out=plane[r:P:32, :, :].bitcast(I32),
+                    in_=ws_view[r][:, :, group * GROUP : (group + 1) * GROUP].bitcast(I32),
+                )
+
+        def load_codes(ci, first, count):
+            n0, width, per = CHUNKS[ci]
+            tiles = []
+            for d in range(first, first + count):
+                wt = codes.tile([P, per, 2 * width], U8, name="wt", tag="wt", align_bytes=64)
+                nc.sync.dma_start(
+                    out=wt[:].bitcast(I32),
+                    in_=W_qk_words[d * per : (d + 1) * per, :, 2 * n0 : 2 * (n0 + width)]
+                    .rearrange("g p n -> p g n")
+                    .bitcast(I32),
+                )
+                tiles.append(wt)
+            return tiles
+
+        nc.sync.dma_start(
+            out=x_codes[:].bitcast(I32), in_=x_words.rearrange("g p n -> p g n").bitcast(I32)
+        )
+        chunk_tiles = {}
+        chunk_tiles[0] = load_codes(0, 0, 2)
+        nc.vector.memset(x_plane[:].bitcast(I32), 0)
+        nc.vector.memset(planes[0][:].bitcast(I32), 0)
+        for r in range(4):
+            nc.sync.dma_start(out=x_plane[r:P:32, :, :].bitcast(I32), in_=xs_view[r].bitcast(I32))
+        load_scales(0)
+        chunk_tiles[0].extend(load_codes(0, 2, 2))
+
+        pos = const.tile([P, 1], F32, name="pos")
+        nc.vector.tensor_copy(out=pos[:], in_=pos_i[:])
+        freq = const.tile([P, HALF], F32, name="freq")
+        nc.vector.memset(freq[:, 0:1], 1.0)
+        ratio = ROPE_BASE ** (-1.0 / HALF)
+        for k in range(7):
+            n = 1 << k
+            nc.vector.tensor_scalar_mul(out=freq[:, n : 2 * n], in0=freq[:, 0:n], scalar1=ratio**n)
+        theta = const.tile([P, HALF], F32, name="theta")
+        nc.vector.tensor_scalar_mul(out=theta[:], in0=freq[:], scalar1=pos[:, 0:1])
+        turns_i = const.tile([P, HALF], I32, name="turns_i")
+        nc.vector.tensor_scalar_mul(out=turns_i[:], in0=theta[:], scalar1=1.0 / (2.0 * PI))
+        turns = const.tile([P, HALF], F32, name="turns")
+        nc.vector.tensor_copy(out=turns[:], in_=turns_i[:])
+        red = const.tile([P, HALF], F32, name="red")
+        nc.vector.scalar_tensor_tensor(
+            out=red[:], in0=turns[:], scalar=-2.0 * PI, in1=theta[:], op0=ALU.mult, op1=ALU.add
+        )
+        shifted = const.tile([P, HALF], F32, name="shifted")
+        nc.vector.tensor_scalar_add(out=shifted[:], in0=red[:], scalar1=PI / 2.0)
+        wrap_s = const.tile([P, HALF], F32, name="wrap_s")
+        nc.vector.tensor_scalar(
+            out=wrap_s[:], in0=red[:], scalar1=PI, scalar2=-2.0 * PI, op0=ALU.is_gt, op1=ALU.mult
+        )
+        wrap_c = const.tile([P, HALF], F32, name="wrap_c")
+        nc.vector.tensor_scalar(
+            out=wrap_c[:], in0=shifted[:], scalar1=PI, scalar2=-2.0 * PI, op0=ALU.is_gt, op1=ALU.mult
+        )
+        arg_s = const.tile([P, HALF], F32, name="arg_s")
+        nc.vector.tensor_tensor(out=arg_s[:], in0=red[:], in1=wrap_s[:], op=ALU.add)
+        arg_c = const.tile([P, HALF], F32, name="arg_c")
+        nc.vector.tensor_tensor(out=arg_c[:], in0=shifted[:], in1=wrap_c[:], op=ALU.add)
+        nc.vector.memset(planes[1][:].bitcast(I32), 0)
+
+        load_scales(1)
+        chunk_tiles[1] = load_codes(1, 0, 4)
+
+        bias = const.tile([P, C_OUT], BF16, name="bias")
+
+        def bias_block(i):
+            pb = psum_b.tile([P, BANK], F32, name="pb", tag="acc")
+            nc.tensor.matmul(
+                pb[:],
+                lhsT=ident[:, i : i + 1].to_broadcast([P, P]),
+                rhs=bias_rows[:],
+                start=True,
+                stop=True,
+            )
+            nc.scalar.copy(out=bias[:, i * BANK : (i + 1) * BANK], in_=pb[:])
+
+        for i in range(8):
+            bias_block(i)
+
+        cos_tab = const.tile([P, BANK], F32, name="cos_tab")
+        sin_tab = const.tile([P, BANK], F32, name="sin_tab")
+        for h in range(BANK // HEAD):
+            lo = h * HEAD
+            nc.scalar.activation(out=cos_tab[:, lo : lo + HALF], in_=arg_c[:], func=ACT.Sin)
+            nc.scalar.activation(out=cos_tab[:, lo + HALF : lo + HEAD], in_=arg_c[:], func=ACT.Sin)
+            nc.scalar.activation(out=sin_tab[:, lo : lo + HALF], in_=arg_s[:], func=ACT.Sin, scale=-1.0)
+            nc.scalar.activation(out=sin_tab[:, lo + HALF : lo + HEAD], in_=arg_s[:], func=ACT.Sin)
+
+        def matmuls(ci, banks, g):
+            n0, width, per = CHUNKS[ci]
+            plane = planes[(n0 // GROUP) % 2]
+            wt = chunk_tiles[ci][g // per]
+            pw = min(width, BANK)
+            for j in range(width // pw):
+                lc = n0 % GROUP + j * pw
+                nc.tensor.matmul_mx(
+                    out=banks[j][:, 0:pw],
+                    lhsT=x_codes[:, g, :].bitcast(FP4X4),
+                    lhsT_scale=x_plane[:, g, :],
+                    rhs=wt[:, g % per, 2 * j * pw : 2 * (j + 1) * pw].bitcast(FP4X4),
+                    rhs_scale=plane[:, g, lc : lc + pw],
+                    start=(g == 0),
+                    stop=(g == PASSES - 1),
+                )
+
+        def halves(ap):
+            return ap.rearrange("p (h u d) -> p h u d", u=2, d=HALF)
+
+        def epilogue(ci, banks):
+            n0, width, per = CHUNKS[ci]
+            pw = min(width, BANK)
+            pieces = width // pw
+            ts = []
+            for j in range(pieces):
+                t = work.tile([P, BANK], F32, name="t", tag="t")
+                c0 = n0 + j * pw
+                nc.vector.tensor_tensor(
+                    out=t[:, 0:pw], in0=banks[j][:, 0:pw], in1=bias[:, c0 : c0 + pw], op=ALU.add
+                )
+                ts.append(t)
+            parts = []
+            for j in range(pieces):
+                t = ts[j]
+                a = work.tile([P, BANK], F32, name="a", tag="a")
+                s = work.tile([P, BANK], F32, name="s", tag="s")
+                nc.vector.tensor_tensor(out=a[:, 0:pw], in0=t[:, 0:pw], in1=cos_tab[:, 0:pw], op=ALU.mult)
+                tv = halves(t[:, 0:pw])
+                sv = halves(s[:, 0:pw])
+                nv = halves(sin_tab[:, 0:pw])
+                nc.vector.tensor_tensor(out=sv[:, :, 0, :], in0=tv[:, :, 1, :], in1=nv[:, :, 0, :], op=ALU.mult)
+                nc.vector.tensor_tensor(out=sv[:, :, 1, :], in0=tv[:, :, 0, :], in1=nv[:, :, 1, :], op=ALU.mult)
+                parts.append((a, s))
+            late = ci >= len(CHUNKS) - LAST_ON_HW_QUEUES
+            per_store = min(pieces, 2)
+            for j0 in range(0, pieces, per_store):
+                o = work.tile([P, 2 * BANK], F32, name="o", tag="o")
+                for j in range(j0, j0 + per_store):
+                    a, s = parts[j]
+                    k0 = (j - j0) * pw
+                    nc.vector.tensor_tensor(out=o[:, k0 : k0 + pw], in0=a[:, 0:pw], in1=s[:, 0:pw], op=ALU.add)
+                c0 = n0 + j0 * pw
+                cols = per_store * pw
+                dst = out_0 if c0 < HALF_OUT else out_1
+                h0 = (c0 % HALF_OUT) // HEAD
+                nh = cols // HEAD
+                for b in range(2):
+                    if late:
+                        eng = nc.sync if b == 0 else nc.scalar
+                    else:
+                        eng = nc.gpsimd
+                    eng.dma_start(
+                        out=dst[b, h0 : h0 + nh, :, :].rearrange("h t d -> t h d"),
+                        in_=o[b * T : (b + 1) * T, 0:cols].rearrange("p (h d) -> p h d", d=HEAD),
+                    )
+
+        for ci in range(len(CHUNKS)):
+            n0, width, per = CHUNKS[ci]
+            pw = min(width, BANK)
+            banks = []
+            for j in range(width // pw):
+                acc = psum[CHUNK_POOL[ci]].tile([P, BANK], F32, name="acc", tag="acc")
+                banks.append(acc)
+            for g in range(PASSES):
+                matmuls(ci, banks, g)
+                if ci == 0 and g in (1, 3):
+                    for i in range(8 + 2 * (g - 1), 12 + 2 * (g - 1)):
+                        bias_block(i)
+            if ci == 0:
+                load_scales(2)
+                chunk_tiles[2] = load_codes(2, 0, 4)
+            if ci == 1:
+                load_scales(3)
+                for cj in range(3, len(CHUNKS)):
+                    chunk_tiles[cj] = load_codes(cj, 0, PASSES // CHUNKS[cj][2])
+            epilogue(ci, banks)

@@ -62,9 +62,10 @@ def tile_causalselfattention_pa_kernel(
         ident = const.tile([P, P], BF16, name="ident")
         make_identity(nc, ident[:])
         pos_i = const.tile([P, 1], I32, name="pos_i")
-        nc.gpsimd.iota(pos_i[0:T, :], pattern=[[1, 1]], base=0, channel_multiplier=1)
-        nc.gpsimd.iota(pos_i[T:P, :], pattern=[[1, 1]], base=0, channel_multiplier=1)
+        nc.gpsimd.iota(pos_i[:], pattern=[[1, 1]], base=0, channel_multiplier=1)
 
+        x_raw = const.tile([P, PASSES, 2 * P], U8, name="x_raw", align_bytes=64)
+        x_plane_raw = const.tile([P, PASSES, P], U8, name="x_plane_raw", align_bytes=64)
         x_codes = const.tile([P, PASSES, 2 * P], U8, name="x_codes", align_bytes=64)
         x_plane = const.tile([P, PASSES, P], U8, name="x_plane", align_bytes=64)
         planes = (
@@ -77,9 +78,9 @@ def tile_causalselfattention_pa_kernel(
         def load_scales(group):
             plane = planes[group % 2]
             for r in range(4):
-                nc.sync.dma_start(
-                    out=plane[r:P:32, :, :].bitcast(I32),
-                    in_=ws_view[r][:, :, group * GROUP : (group + 1) * GROUP].bitcast(I32),
+                nc.gpsimd.dma_start(
+                    out=plane[r:P:32, :, :].bitcast(F32),
+                    in_=ws_view[r][:, :, group * GROUP : (group + 1) * GROUP].bitcast(F32),
                 )
 
         def load_codes(ci, first, count):
@@ -97,19 +98,30 @@ def tile_causalselfattention_pa_kernel(
             return tiles
 
         nc.sync.dma_start(
-            out=x_codes[:].bitcast(I32), in_=x_words.rearrange("g p n -> p g n").bitcast(I32)
+            out=x_raw[:].bitcast(I32), in_=x_words.rearrange("g p n -> p g n").bitcast(I32)
         )
         chunk_tiles = {}
         chunk_tiles[0] = load_codes(0, 0, 2)
-        nc.vector.memset(x_plane[:].bitcast(I32), 0)
+        nc.vector.memset(x_plane_raw[:].bitcast(I32), 0)
         nc.vector.memset(planes[0][:].bitcast(I32), 0)
         for r in range(4):
-            nc.sync.dma_start(out=x_plane[r:P:32, :, :].bitcast(I32), in_=xs_view[r].bitcast(I32))
+            nc.sync.dma_start(out=x_plane_raw[r:P:32, :, :].bitcast(I32), in_=xs_view[r].bitcast(I32))
         load_scales(0)
         chunk_tiles[0].extend(load_codes(0, 2, 2))
+        for g in range(PASSES):
+            nc.vector.tensor_copy(
+                out=x_codes[:, g, :].rearrange("p (t b e) -> p t b e", b=2, e=2),
+                in_=x_raw[:, g, :].rearrange("p (b t e) -> p t b e", b=2, e=2),
+            )
+        nc.vector.tensor_copy(
+            out=x_plane[:].rearrange("p g (t b) -> p g t b", b=2),
+            in_=x_plane_raw[:].rearrange("p g (b t) -> p g t b", b=2),
+        )
 
+        half_i = const.tile([P, 1], I32, name="half_i")
+        nc.vector.tensor_single_scalar(out=half_i[:], in_=pos_i[:], scalar=1, op=ALU.arith_shift_right)
         pos = const.tile([P, 1], F32, name="pos")
-        nc.vector.tensor_copy(out=pos[:], in_=pos_i[:])
+        nc.vector.tensor_copy(out=pos[:], in_=half_i[:])
         freq = const.tile([P, HALF], F32, name="freq")
         nc.vector.memset(freq[:, 0:1], 1.0)
         ratio = ROPE_BASE ** (-1.0 / HALF)
@@ -234,7 +246,7 @@ def tile_causalselfattention_pa_kernel(
                         eng = nc.gpsimd
                     eng.dma_start(
                         out=dst[b, h0 : h0 + nh, :, :].rearrange("h t d -> t h d"),
-                        in_=o[b * T : (b + 1) * T, 0:cols].rearrange("p (h d) -> p h d", d=HEAD),
+                        in_=o[b:P:2, 0:cols].rearrange("p (h d) -> p h d", d=HEAD),
                     )
 
         for ci in range(len(CHUNKS)):

@@ -28,13 +28,15 @@ FLOPS = 2 * 128 * 4096 * 8192
 CHUNKS = (
     (0, 2048, 2),
     (2048, 2048, 2),
-    (4096, 2048, 2),
+    (4096, 1024, 4),
+    (5120, 1024, 4),
     (6144, 1024, 4),
     (7168, 512, 4),
     (7680, 256, 8),
     (7936, 256, 4),
 )
-CHUNK_POOL = (0, 1, 0, 1, 1, 1, 0)
+CHUNK_POOL = (0, 1, 0, 0, 1, 1, 1, 0)
+LOADS_AFTER = {0: (3, 4), 1: (5, 6), 2: (7,)}
 LAST_ON_HW_QUEUES = 2
 
 
@@ -44,7 +46,7 @@ def tile_causalselfattention_pa_kernel(
     nc = tc.nc
     with ExitStack() as ctx:
         const = ctx.enter_context(tc.tile_pool(name="const", bufs=1))
-        codes = ctx.enter_context(tc.tile_pool(name="codes", bufs=12))
+        codes = ctx.enter_context(tc.tile_pool(name="codes", bufs=10))
         work = ctx.enter_context(tc.tile_pool(name="work", bufs=4))
         psum_a = ctx.enter_context(tc.psum_pool(name="psum_a", bufs=4))
         psum_b = ctx.enter_context(tc.psum_pool(name="psum_b", bufs=4))
@@ -71,17 +73,20 @@ def tile_causalselfattention_pa_kernel(
         planes = (
             const.tile([P, PASSES, GROUP], U8, name="plane0", align_bytes=64),
             const.tile([P, PASSES, GROUP], U8, name="plane1", align_bytes=64),
+            const.tile([P, PASSES, GROUP], U8, name="plane2", align_bytes=64),
+            const.tile([P, PASSES, GROUP], U8, name="plane3", align_bytes=64),
         )
         xs_view = x_scales.rearrange("g (q r) n -> r q g n", r=4)
         ws_view = W_qk_scales.rearrange("g (q r) n -> r q g n", r=4)
 
         def load_scales(group):
-            plane = planes[group % 2]
-            for r in range(4):
-                nc.gpsimd.dma_start(
-                    out=plane[r:P:32, :, :].bitcast(F32),
-                    in_=ws_view[r][:, :, group * GROUP : (group + 1) * GROUP].bitcast(F32),
-                )
+            plane = planes[group]
+            for g0 in (0, 4):
+                for r in range(4):
+                    nc.sync.dma_start(
+                        out=plane[r:P:32, g0 : g0 + 4, :].bitcast(I32),
+                        in_=ws_view[r][:, g0 : g0 + 4, group * GROUP : (group + 1) * GROUP].bitcast(I32),
+                    )
 
         def load_codes(ci, first, count):
             n0, width, per = CHUNKS[ci]
@@ -101,13 +106,16 @@ def tile_causalselfattention_pa_kernel(
             out=x_raw[:].bitcast(I32), in_=x_words.rearrange("g p n -> p g n").bitcast(I32)
         )
         chunk_tiles = {}
-        chunk_tiles[0] = load_codes(0, 0, 2)
         nc.vector.memset(x_plane_raw[:].bitcast(I32), 0)
         nc.vector.memset(planes[0][:].bitcast(I32), 0)
+        nc.vector.memset(planes[1][:].bitcast(I32), 0)
         for r in range(4):
             nc.sync.dma_start(out=x_plane_raw[r:P:32, :, :].bitcast(I32), in_=xs_view[r].bitcast(I32))
+        chunk_tiles[0] = load_codes(0, 0, 1)
         load_scales(0)
-        chunk_tiles[0].extend(load_codes(0, 2, 2))
+        load_scales(1)
+        chunk_tiles[0].extend(load_codes(0, 1, 3))
+        chunk_tiles[1] = load_codes(1, 0, 4)
         for g in range(PASSES):
             nc.vector.tensor_copy(
                 out=x_codes[:, g, :].rearrange("p (t b e) -> p t b e", b=2, e=2),
@@ -152,10 +160,11 @@ def tile_causalselfattention_pa_kernel(
         nc.vector.tensor_tensor(out=arg_s[:], in0=red[:], in1=wrap_s[:], op=ALU.add)
         arg_c = const.tile([P, HALF], F32, name="arg_c")
         nc.vector.tensor_tensor(out=arg_c[:], in0=shifted[:], in1=wrap_c[:], op=ALU.add)
-        nc.vector.memset(planes[1][:].bitcast(I32), 0)
-
-        load_scales(1)
-        chunk_tiles[1] = load_codes(1, 0, 4)
+        nc.vector.memset(planes[2][:].bitcast(I32), 0)
+        nc.vector.memset(planes[3][:].bitcast(I32), 0)
+        load_scales(2)
+        load_scales(3)
+        chunk_tiles[2] = load_codes(2, 0, 2)
 
         bias = const.tile([P, C_OUT], BF16, name="bias")
 
@@ -184,7 +193,7 @@ def tile_causalselfattention_pa_kernel(
 
         def matmuls(ci, banks, g):
             n0, width, per = CHUNKS[ci]
-            plane = planes[(n0 // GROUP) % 2]
+            plane = planes[n0 // GROUP]
             wt = chunk_tiles[ci][g // per]
             pw = min(width, BANK)
             for j in range(width // pw):
@@ -261,11 +270,6 @@ def tile_causalselfattention_pa_kernel(
                 if ci == 0 and g in (1, 3):
                     for i in range(8 + 2 * (g - 1), 12 + 2 * (g - 1)):
                         bias_block(i)
-            if ci == 0:
-                load_scales(2)
-                chunk_tiles[2] = load_codes(2, 0, 4)
-            if ci == 1:
-                load_scales(3)
-                for cj in range(3, len(CHUNKS)):
-                    chunk_tiles[cj] = load_codes(cj, 0, PASSES // CHUNKS[cj][2])
+            for cj in LOADS_AFTER.get(ci, ()):
+                chunk_tiles[cj] = load_codes(cj, 0, PASSES // CHUNKS[cj][2])
             epilogue(ci, banks)

@@ -28,16 +28,13 @@ FLOPS = 2 * 128 * 4096 * 8192
 CHUNKS = (
     (0, 2048, 2),
     (2048, 2048, 2),
-    (4096, 1024, 4),
-    (5120, 1024, 4),
+    (4096, 2048, 2),
     (6144, 1024, 4),
-    (7168, 512, 4),
-    (7680, 256, 8),
-    (7936, 256, 4),
+    (7168, 1024, 4),
 )
-CHUNK_POOL = (0, 1, 0, 0, 1, 1, 1, 0)
-LOADS_AFTER = {0: (3, 4), 1: (5, 6), 2: (7,)}
-LAST_ON_HW_QUEUES = 2
+CHUNK_POOL = (0, 1, 0, 1, 1)
+LOADS_AFTER = {0: (2, (2,)), 1: (3, (3, 4))}
+STORE = 1024
 
 
 def tile_causalselfattention_pa_kernel(
@@ -73,14 +70,12 @@ def tile_causalselfattention_pa_kernel(
         planes = (
             const.tile([P, PASSES, GROUP], U8, name="plane0", align_bytes=64),
             const.tile([P, PASSES, GROUP], U8, name="plane1", align_bytes=64),
-            const.tile([P, PASSES, GROUP], U8, name="plane2", align_bytes=64),
-            const.tile([P, PASSES, GROUP], U8, name="plane3", align_bytes=64),
         )
         xs_view = x_scales.rearrange("g (q r) n -> r q g n", r=4)
         ws_view = W_qk_scales.rearrange("g (q r) n -> r q g n", r=4)
 
         def load_scales(group):
-            plane = planes[group]
+            plane = planes[group % 2]
             for g0 in (0, 4):
                 for r in range(4):
                     nc.sync.dma_start(
@@ -160,11 +155,6 @@ def tile_causalselfattention_pa_kernel(
         nc.vector.tensor_tensor(out=arg_s[:], in0=red[:], in1=wrap_s[:], op=ALU.add)
         arg_c = const.tile([P, HALF], F32, name="arg_c")
         nc.vector.tensor_tensor(out=arg_c[:], in0=shifted[:], in1=wrap_c[:], op=ALU.add)
-        nc.vector.memset(planes[2][:].bitcast(I32), 0)
-        nc.vector.memset(planes[3][:].bitcast(I32), 0)
-        load_scales(2)
-        load_scales(3)
-        chunk_tiles[2] = load_codes(2, 0, 2)
 
         bias = const.tile([P, C_OUT], BF16, name="bias")
 
@@ -193,7 +183,7 @@ def tile_causalselfattention_pa_kernel(
 
         def matmuls(ci, banks, g):
             n0, width, per = CHUNKS[ci]
-            plane = planes[n0 // GROUP]
+            plane = planes[(n0 // GROUP) % 2]
             wt = chunk_tiles[ci][g // per]
             pw = min(width, BANK)
             for j in range(width // pw):
@@ -235,29 +225,30 @@ def tile_causalselfattention_pa_kernel(
                 nc.vector.tensor_tensor(out=sv[:, :, 0, :], in0=tv[:, :, 1, :], in1=nv[:, :, 0, :], op=ALU.mult)
                 nc.vector.tensor_tensor(out=sv[:, :, 1, :], in0=tv[:, :, 0, :], in1=nv[:, :, 1, :], op=ALU.mult)
                 parts.append((a, s))
-            late = ci >= len(CHUNKS) - LAST_ON_HW_QUEUES
-            per_store = min(pieces, 2)
-            for j0 in range(0, pieces, per_store):
-                o = work.tile([P, 2 * BANK], F32, name="o", tag="o")
-                for j in range(j0, j0 + per_store):
-                    a, s = parts[j]
-                    k0 = (j - j0) * pw
-                    nc.vector.tensor_tensor(out=o[:, k0 : k0 + pw], in0=a[:, 0:pw], in1=s[:, 0:pw], op=ALU.add)
-                c0 = n0 + j0 * pw
-                cols = per_store * pw
-                dst = out_0 if c0 < HALF_OUT else out_1
-                h0 = (c0 % HALF_OUT) // HEAD
-                nh = cols // HEAD
-                for b in range(2):
-                    if late:
-                        eng = nc.sync if b == 0 else nc.scalar
-                    else:
-                        eng = nc.gpsimd
-                    eng.dma_start(
-                        out=dst[b, h0 : h0 + nh, :, :].rearrange("h t d -> t h d"),
-                        in_=o[b:P:2, 0:cols].rearrange("p (h d) -> p h d", d=HEAD),
-                    )
+            for j in range(pieces):
+                a, s = parts[j]
+                c0 = n0 + j * pw
+                o = outs[c0 // STORE]
+                k0 = c0 % STORE
+                nc.vector.tensor_tensor(out=o[:, k0 : k0 + pw], in0=a[:, 0:pw], in1=s[:, 0:pw], op=ALU.add)
+            return list(range(n0 // STORE, (n0 + width) // STORE))
 
+        def store(i):
+            c0 = i * STORE
+            dst = out_0 if c0 < HALF_OUT else out_1
+            h0 = (c0 % HALF_OUT) // HEAD
+            nh = STORE // HEAD
+            for b in range(2):
+                nc.sync.dma_start(
+                    out=dst[b, h0 : h0 + nh, :, :].rearrange("h t d -> t h d"),
+                    in_=outs[i][b:P:2, :].rearrange("p (h d) -> p h d", d=HEAD),
+                )
+
+        outs = []
+        for i in range(C_OUT // STORE):
+            o_tile = const.tile([P, STORE], F32, name="o%d" % i)
+            outs.append(o_tile)
+        pending = []
         for ci in range(len(CHUNKS)):
             n0, width, per = CHUNKS[ci]
             pw = min(width, BANK)
@@ -270,6 +261,13 @@ def tile_causalselfattention_pa_kernel(
                 if ci == 0 and g in (1, 3):
                     for i in range(8 + 2 * (g - 1), 12 + 2 * (g - 1)):
                         bias_block(i)
-            for cj in LOADS_AFTER.get(ci, ()):
-                chunk_tiles[cj] = load_codes(cj, 0, PASSES // CHUNKS[cj][2])
-            epilogue(ci, banks)
+            if ci in LOADS_AFTER:
+                group, later = LOADS_AFTER[ci]
+                load_scales(group)
+                for cj in later:
+                    chunk_tiles[cj] = load_codes(cj, 0, PASSES // CHUNKS[cj][2])
+            pending.extend(epilogue(ci, banks))
+            if ci >= max(LOADS_AFTER):
+                for i in pending:
+                    store(i)
+                pending.clear()

@@ -72,15 +72,15 @@ def tile_causalselfattention_pa_kernel(
             const.tile([P, PASSES, GROUP], U8, name="plane1", align_bytes=64),
         )
         xs_view = x_scales.rearrange("g (q r) n -> r q g n", r=4)
-        ws_view = W_qk_scales.rearrange("g (q r) n -> r q g n", r=4)
+        ws_view = W_qk_scales.rearrange("g (u a r) n -> a r u g n", u=2, a=2, r=4)
 
         def load_scales(group):
             plane = planes[group % 2]
-            for g0 in (0, 4):
+            for a in range(2):
                 for r in range(4):
                     nc.sync.dma_start(
-                        out=plane[r:P:32, g0 : g0 + 4, :].bitcast(I32),
-                        in_=ws_view[r][:, g0 : g0 + 4, group * GROUP : (group + 1) * GROUP].bitcast(I32),
+                        out=plane[32 * a + r : P : 64, :, :].bitcast(I32),
+                        in_=ws_view[a, r, :, :, group * GROUP : (group + 1) * GROUP].bitcast(I32),
                     )
 
         def load_codes(ci, first, count):

from contextlib import ExitStack

import concourse.mybir as mybir
from concourse.masks import make_identity

F32 = mybir.dt.float32
BF16 = mybir.dt.bfloat16
I32 = mybir.dt.int32
U8 = mybir.dt.uint8
FP4X4 = mybir.dt.float4_e2m1fn_x4
ALU = mybir.AluOpType
ACT = mybir.ActivationFunctionType

P = 128
PASSES = 8
C_OUT = 8192
HALF_OUT = 4096
HEAD = 256
HALF = 128
BANK = 512
GROUP = 2048
T = 64
PI = 3.141592653589793
ROPE_BASE = 10000.0

FLOPS = 2 * 128 * 4096 * 8192

CHUNKS = (
    (0, 2048, 2),
    (2048, 2048, 2),
    (4096, 2048, 2),
    (6144, 1024, 4),
    (7168, 1024, 4),
)
CHUNK_POOL = (0, 1, 0, 1, 1)
LOADS_AFTER = {0: (2, (2,)), 1: (3, (3, 4))}
STORE = 1024


def tile_causalselfattention_pa_kernel(
    tc, x_words, x_scales, W_qk_words, W_qk_scales, b_qk, out_0, out_1
):
    nc = tc.nc
    with ExitStack() as ctx:
        const = ctx.enter_context(tc.tile_pool(name="const", bufs=1))
        codes = ctx.enter_context(tc.tile_pool(name="codes", bufs=10))
        work = ctx.enter_context(tc.tile_pool(name="work", bufs=4))
        psum_a = ctx.enter_context(tc.psum_pool(name="psum_a", bufs=4))
        psum_b = ctx.enter_context(tc.psum_pool(name="psum_b", bufs=4))
        psum = (psum_a, psum_b)
        ctx.enter_context(tc.manual_schedule())

        bias_rows = const.tile([P, BANK], BF16, name="bias_rows")
        nc.vector.memset(bias_rows[:], 0.0)
        nc.scalar.dma_start(out=bias_rows[0:16, :], in_=b_qk.rearrange("(a n) -> a n", a=16))
        zero_col = const.tile([P, 1], F32, name="zero_col")
        nc.vector.memset(zero_col[:], 0.0)
        warm = const.tile([P, 1], F32, name="warm")
        nc.scalar.activation(out=warm[:], in_=zero_col[:], func=ACT.Sin)

        ident = const.tile([P, P], BF16, name="ident")
        make_identity(nc, ident[:])
        pos_i = const.tile([P, 1], I32, name="pos_i")
        nc.gpsimd.iota(pos_i[:], pattern=[[1, 1]], base=0, channel_multiplier=1)

        x_raw = const.tile([P, PASSES, 2 * P], U8, name="x_raw", align_bytes=64)
        x_plane_raw = const.tile([P, PASSES, P], U8, name="x_plane_raw", align_bytes=64)
        x_codes = const.tile([P, PASSES, 2 * P], U8, name="x_codes", align_bytes=64)
        x_plane = const.tile([P, PASSES, P], U8, name="x_plane", align_bytes=64)
        planes = (
            const.tile([P, PASSES, GROUP], U8, name="plane0", align_bytes=64),
            const.tile([P, PASSES, GROUP], U8, name="plane1", align_bytes=64),
        )
        xs_view = x_scales.rearrange("g (q r) n -> r q g n", r=4)
        ws_view = W_qk_scales.rearrange("g (u a r) n -> a r u g n", u=2, a=2, r=4)

        def load_scales(group):
            plane = planes[group % 2]
            for a in range(2):
                for r in range(4):
                    nc.sync.dma_start(
                        out=plane[32 * a + r : P : 64, :, :].bitcast(I32),
                        in_=ws_view[a, r, :, :, group * GROUP : (group + 1) * GROUP].bitcast(I32),
                    )

        def load_codes(ci, first, count):
            n0, width, per = CHUNKS[ci]
            tiles = []
            for d in range(first, first + count):
                wt = codes.tile([P, per, 2 * width], U8, name="wt", tag="wt", align_bytes=64)
                nc.sync.dma_start(
                    out=wt[:].bitcast(I32),
                    in_=W_qk_words[d * per : (d + 1) * per, :, 2 * n0 : 2 * (n0 + width)]
                    .rearrange("g p n -> p g n")
                    .bitcast(I32),
                )
                tiles.append(wt)
            return tiles

        nc.sync.dma_start(
            out=x_raw[:].bitcast(I32), in_=x_words.rearrange("g p n -> p g n").bitcast(I32)
        )
        chunk_tiles = {}
        nc.vector.memset(x_plane_raw[:].bitcast(I32), 0)
        nc.vector.memset(planes[0][:].bitcast(I32), 0)
        nc.vector.memset(planes[1][:].bitcast(I32), 0)
        for r in range(4):
            nc.sync.dma_start(out=x_plane_raw[r:P:32, :, :].bitcast(I32), in_=xs_view[r].bitcast(I32))
        chunk_tiles[0] = load_codes(0, 0, 1)
        load_scales(0)
        load_scales(1)
        chunk_tiles[0].extend(load_codes(0, 1, 3))
        chunk_tiles[1] = load_codes(1, 0, 4)
        for g in range(PASSES):
            nc.vector.tensor_copy(
                out=x_codes[:, g, :].rearrange("p (t b e) -> p t b e", b=2, e=2),
                in_=x_raw[:, g, :].rearrange("p (b t e) -> p t b e", b=2, e=2),
            )
        nc.vector.tensor_copy(
            out=x_plane[:].rearrange("p g (t b) -> p g t b", b=2),
            in_=x_plane_raw[:].rearrange("p g (b t) -> p g t b", b=2),
        )

        half_i = const.tile([P, 1], I32, name="half_i")
        nc.vector.tensor_single_scalar(out=half_i[:], in_=pos_i[:], scalar=1, op=ALU.arith_shift_right)
        pos = const.tile([P, 1], F32, name="pos")
        nc.vector.tensor_copy(out=pos[:], in_=half_i[:])
        freq = const.tile([P, HALF], F32, name="freq")
        nc.vector.memset(freq[:, 0:1], 1.0)
        ratio = ROPE_BASE ** (-1.0 / HALF)
        for k in range(7):
            n = 1 << k
            nc.vector.tensor_scalar_mul(out=freq[:, n : 2 * n], in0=freq[:, 0:n], scalar1=ratio**n)
        theta = const.tile([P, HALF], F32, name="theta")
        nc.vector.tensor_scalar_mul(out=theta[:], in0=freq[:], scalar1=pos[:, 0:1])
        turns_i = const.tile([P, HALF], I32, name="turns_i")
        nc.vector.tensor_scalar_mul(out=turns_i[:], in0=theta[:], scalar1=1.0 / (2.0 * PI))
        turns = const.tile([P, HALF], F32, name="turns")
        nc.vector.tensor_copy(out=turns[:], in_=turns_i[:])
        red = const.tile([P, HALF], F32, name="red")
        nc.vector.scalar_tensor_tensor(
            out=red[:], in0=turns[:], scalar=-2.0 * PI, in1=theta[:], op0=ALU.mult, op1=ALU.add
        )
        shifted = const.tile([P, HALF], F32, name="shifted")
        nc.vector.tensor_scalar_add(out=shifted[:], in0=red[:], scalar1=PI / 2.0)
        wrap_s = const.tile([P, HALF], F32, name="wrap_s")
        nc.vector.tensor_scalar(
            out=wrap_s[:], in0=red[:], scalar1=PI, scalar2=-2.0 * PI, op0=ALU.is_gt, op1=ALU.mult
        )
        wrap_c = const.tile([P, HALF], F32, name="wrap_c")
        nc.vector.tensor_scalar(
            out=wrap_c[:], in0=shifted[:], scalar1=PI, scalar2=-2.0 * PI, op0=ALU.is_gt, op1=ALU.mult
        )
        arg_s = const.tile([P, HALF], F32, name="arg_s")
        nc.vector.tensor_tensor(out=arg_s[:], in0=red[:], in1=wrap_s[:], op=ALU.add)
        arg_c = const.tile([P, HALF], F32, name="arg_c")
        nc.vector.tensor_tensor(out=arg_c[:], in0=shifted[:], in1=wrap_c[:], op=ALU.add)

        bias = const.tile([P, C_OUT], BF16, name="bias")

        def bias_block(i):
            pb = psum_b.tile([P, BANK], F32, name="pb", tag="acc")
            nc.tensor.matmul(
                pb[:],
                lhsT=ident[:, i : i + 1].to_broadcast([P, P]),
                rhs=bias_rows[:],
                start=True,
                stop=True,
            )
            nc.scalar.copy(out=bias[:, i * BANK : (i + 1) * BANK], in_=pb[:])

        for i in range(8):
            bias_block(i)

        cos_tab = const.tile([P, BANK], F32, name="cos_tab")
        sin_tab = const.tile([P, BANK], F32, name="sin_tab")
        for h in range(BANK // HEAD):
            lo = h * HEAD
            nc.scalar.activation(out=cos_tab[:, lo : lo + HALF], in_=arg_c[:], func=ACT.Sin)
            nc.scalar.activation(out=cos_tab[:, lo + HALF : lo + HEAD], in_=arg_c[:], func=ACT.Sin)
            nc.scalar.activation(out=sin_tab[:, lo : lo + HALF], in_=arg_s[:], func=ACT.Sin, scale=-1.0)
            nc.scalar.activation(out=sin_tab[:, lo + HALF : lo + HEAD], in_=arg_s[:], func=ACT.Sin)

        def matmuls(ci, banks, g):
            n0, width, per = CHUNKS[ci]
            plane = planes[(n0 // GROUP) % 2]
            wt = chunk_tiles[ci][g // per]
            pw = min(width, BANK)
            for j in range(width // pw):
                lc = n0 % GROUP + j * pw
                nc.tensor.matmul_mx(
                    out=banks[j][:, 0:pw],
                    lhsT=x_codes[:, g, :].bitcast(FP4X4),
                    lhsT_scale=x_plane[:, g, :],
                    rhs=wt[:, g % per, 2 * j * pw : 2 * (j + 1) * pw].bitcast(FP4X4),
                    rhs_scale=plane[:, g, lc : lc + pw],
                    start=(g == 0),
                    stop=(g == PASSES - 1),
                )

        def halves(ap):
            return ap.rearrange("p (h u d) -> p h u d", u=2, d=HALF)

        def epilogue(ci, banks):
            n0, width, per = CHUNKS[ci]
            pw = min(width, BANK)
            pieces = width // pw
            ts = []
            for j in range(pieces):
                t = work.tile([P, BANK], F32, name="t", tag="t")
                c0 = n0 + j * pw
                nc.vector.tensor_tensor(
                    out=t[:, 0:pw], in0=banks[j][:, 0:pw], in1=bias[:, c0 : c0 + pw], op=ALU.add
                )
                ts.append(t)
            parts = []
            for j in range(pieces):
                t = ts[j]
                a = work.tile([P, BANK], F32, name="a", tag="a")
                s = work.tile([P, BANK], F32, name="s", tag="s")
                nc.vector.tensor_tensor(out=a[:, 0:pw], in0=t[:, 0:pw], in1=cos_tab[:, 0:pw], op=ALU.mult)
                tv = halves(t[:, 0:pw])
                sv = halves(s[:, 0:pw])
                nv = halves(sin_tab[:, 0:pw])
                nc.vector.tensor_tensor(out=sv[:, :, 0, :], in0=tv[:, :, 1, :], in1=nv[:, :, 0, :], op=ALU.mult)
                nc.vector.tensor_tensor(out=sv[:, :, 1, :], in0=tv[:, :, 0, :], in1=nv[:, :, 1, :], op=ALU.mult)
                parts.append((a, s))
            for j in range(pieces):
                a, s = parts[j]
                c0 = n0 + j * pw
                o = outs[c0 // STORE]
                k0 = c0 % STORE
                nc.vector.tensor_tensor(out=o[:, k0 : k0 + pw], in0=a[:, 0:pw], in1=s[:, 0:pw], op=ALU.add)
            return list(range(n0 // STORE, (n0 + width) // STORE))

        def store(i):
            c0 = i * STORE
            dst = out_0 if c0 < HALF_OUT else out_1
            h0 = (c0 % HALF_OUT) // HEAD
            nh = STORE // HEAD
            for b in range(2):
                nc.sync.dma_start(
                    out=dst[b, h0 : h0 + nh, :, :].rearrange("h t d -> t h d"),
                    in_=outs[i][b:P:2, :].rearrange("p (h d) -> p h d", d=HEAD),
                )

        outs = []
        for i in range(C_OUT // STORE):
            o_tile = const.tile([P, STORE], F32, name="o%d" % i)
            outs.append(o_tile)
        pending = []
        for ci in range(len(CHUNKS)):
            n0, width, per = CHUNKS[ci]
            pw = min(width, BANK)
            banks = []
            for j in range(width // pw):
                acc = psum[CHUNK_POOL[ci]].tile([P, BANK], F32, name="acc", tag="acc")
                banks.append(acc)
            for g in range(PASSES):
                matmuls(ci, banks, g)
                if ci == 0 and g in (1, 3):
                    for i in range(8 + 2 * (g - 1), 12 + 2 * (g - 1)):
                        bias_block(i)
            if ci in LOADS_AFTER:
                group, later = LOADS_AFTER[ci]
                load_scales(group)
                for cj in later:
                    chunk_tiles[cj] = load_codes(cj, 0, PASSES // CHUNKS[cj][2])
            pending.extend(epilogue(ci, banks))
            if ci >= max(LOADS_AFTER):
                for i in pending:
                    store(i)
                pending.clear()
